import numpy as np
import ml_dtypes


def mxq(x, axis, fmt="e4m3"):
    dtype, down = {"e4m3": (ml_dtypes.float8_e4m3fn, 7), "e5m2": (ml_dtypes.float8_e5m2, 14)}[fmt]
    v = np.moveaxis(np.asarray(x, np.float32).astype(ml_dtypes.bfloat16).astype(np.float64), axis, -1)
    blocks = v.reshape(v.shape[:-1] + (-1, 32))
    amax = np.abs(blocks).max(-1, keepdims=True)
    byte = np.maximum(np.where(amax > 0, np.frexp(amax)[1] - 1 + 127, 0) - down, 1)
    scale = np.exp2(byte - 127.0)
    codes = (blocks / scale).astype(np.float32).astype(dtype).astype(np.float64)
    return np.moveaxis((codes * scale).reshape(v.shape), -1, axis)


WIDE = False


def mx_kscale(k):
    if not WIDE:
        return np.ones(k)
    levels = np.array([10, -10, 5, -5, 0])
    a = np.random.permutation(np.resize(levels, k // 512 * 4)).reshape(k // 512, 4)
    idx = np.arange(k)
    return np.exp2(a[idx // 512, idx % 128 // 32])


BF16 = ml_dtypes.bfloat16


def bf(x):
    return np.asarray(x, np.float32).astype(BF16)


def f64(x):
    return np.asarray(x).astype(np.float64)


B, C, P, NH, NW = 4, 8, 8, 32, 32
D = C * P * P
QK_SCALE = 1.0


def rel_bias(p):
    i = np.arange(p, dtype=np.float64)
    down = np.exp(-i / (p / 2))[:, None] * np.ones((1, p))
    right = down.T
    br = np.exp(-(i[:, None] + i[None, :]) / (p / 2))
    return np.stack([
        np.rot90(br, 2), np.flip(down, 0), np.rot90(br, 1),
        np.flip(right, 1), np.ones((p, p)), right,
        np.rot90(br, 3), down, br,
    ], axis=0)


def setup_inputs():
    s = mx_kscale(D)
    sx = np.tile(s.reshape(C, P, P), (1, NH, NW))
    return {"x": bf(np.random.standard_normal((B, C, NH * P, NW * P)) * sx),
            "W_qkv": bf(np.random.standard_normal((3 * D, D)) / np.sqrt(D) / s),
            "b_qkv": bf(np.random.standard_normal(3 * D) * 0.5)}


def reference(x, W_qkv, b_qkv):
    p, c = P, C
    b, _, h, w = x.shape
    nh, nw = h // p, w // p
    feat = f64(x).reshape(b, c, nh, p, nw, p).transpose(0, 2, 4, 1, 3, 5).reshape(b, nh, nw, c * p * p)
    y = mxq(feat, 3, "e4m3") @ mxq(f64(W_qkv), 1, "e4m3").T
    qkv = np.pad(y, ((0, 0), (1, 1), (1, 1), (0, 0))) + f64(b_qkv)
    qkv = qkv.reshape(b, nh + 2, nw + 2, 3, c, p, p)
    core_q = qkv[:, 1:nh + 1, 1:nw + 1, 0] * QK_SCALE
    k = np.stack([qkv[:, di:di + nh, dj:dj + nw, 1] for di in range(3) for dj in range(3)], axis=3)
    v = np.stack([qkv[:, di:di + nh, dj:dj + nw, 2] for di in range(3) for dj in range(3)], axis=3)
    bias = rel_bias(p)
    attn = core_q[:, :, :, None] * k * bias[:, None]
    out = np.sum(attn * v, axis=3)
    return out.transpose(0, 3, 1, 4, 2, 5).reshape(b, c, nh * p, nw * p)

@@ -1,0 +1,252 @@
+from contextlib import ExitStack
+
+import concourse.mybir as mybir
+from concourse.masks import make_identity
+
+F32 = mybir.dt.float32
+BF16 = mybir.dt.bfloat16
+U32 = mybir.dt.uint32
+U8 = mybir.dt.uint8
+FP8X4 = mybir.dt.float8_e4m3fn_x4
+ADD = mybir.AluOpType.add
+MULT = mybir.AluOpType.mult
+IDENTITY = mybir.ActivationFunctionType.Identity
+EXP = mybir.ActivationFunctionType.Exp
+
+FLOPS = 2 * 4096 * 512 * 1536
+
+P = 128
+NB = 4
+NJ = 32
+NG = 8
+NF = 4
+ROW = 132
+
+
+def tile_attentionconv_t_kernel(tc, x, W_qkv, b_qkv, out):
+    nc = tc.nc
+    with ExitStack() as ctx:
+        keep = ctx.enter_context(tc.tile_pool(name="keep", bufs=1))
+        work = ctx.enter_context(tc.tile_pool(name="work", bufs=2))
+        psum = ctx.enter_context(tc.psum_pool(name="psum", bufs=2))
+
+        ident = keep.tile([P, P], F32, name="ident")
+        make_identity(nc, ident[:])
+        zero = keep.tile([P, ROW], F32, name="zero")
+        nc.vector.memset(zero[:], 0.0)
+        zs = keep.tile([P, P], F32, name="zs")
+        zr = keep.tile([P, P], F32, name="zr")
+        for t in range(8):
+            nc.vector.memset(zs[:].rearrange("p (a s) -> p a s", s=8)[:, :, t : t + 1], float(-t))
+            nc.gpsimd.memset(zr[:].rearrange("p (c r s) -> p c r s", c=2, r=8)[:, :, t : t + 1, :], float(-t))
+        bz = keep.tile([P, P], BF16, name="bz")
+        nc.vector.memset(bz[:], 0.0)
+        nc.sync.dma_start(out=bz[0:12, :], in_=b_qkv.rearrange("(s p) -> s p", p=P))
+
+        w_sb = keep.tile([P, 12 * 512], BF16, name="w_sb")
+        w_view = W_qkv.rearrange("(t f p) e -> f p t e", t=3, f=NF, p=P)
+
+        def load_w(fb):
+            nc.sync.dma_start(
+                out=w_sb[:, fb * 1536 : (fb + 1) * 1536].rearrange("p (t e) -> p t e", t=3), in_=w_view[fb]
+            )
+
+        load_w(0)
+        xs = work.tile([P, 16384], BF16, name="xs", tag="big", bufs=2)
+        for cp in range(4):
+            for b in range(NB):
+                nc.sync.dma_start(
+                    out=xs[b:P:4, cp * 4096 : (cp + 1) * 4096].rearrange("p (c f) -> p c f", c=2),
+                    in_=x[b, 2 * cp : 2 * cp + 2].rearrange("c (i r) w -> i c (r w)", r=8),
+                )
+        for fb in range(1, NF):
+            load_w(fb)
+
+        bzf = keep.tile([P, P], F32, name="bzf")
+        nc.vector.tensor_copy(out=bzf[:], in_=bz[:])
+        cps = psum.tile([P, 512], F32, name="cps", tag="tp", bufs=2)
+        nc.tensor.transpose(cps[:, 0:P], zs[:], ident[:])
+        nc.tensor.transpose(cps[:, P : 2 * P], zr[:], ident[:])
+        bps = psum.tile([P, 512], F32, name="bps", tag="tp", bufs=2)
+        nc.tensor.transpose(bps[:, 0:P], bzf[:], ident[:])
+        consts = keep.tile([P, 12], F32, name="consts")
+        nc.vector.tensor_copy(out=consts[:, 0:12], in_=bps[:, 0:12])
+        expo = keep.tile([P, 4], F32, name="expo")
+        nc.vector.tensor_copy(
+            out=expo[:, 0:2].unsqueeze(2), in_=cps[:, 0 : 2 * P].rearrange("p (w c) -> p w c", c=P)[:, :, 0:1]
+        )
+        nc.vector.tensor_scalar(
+            out=expo[:, 2:4], in0=expo[:, 0:2], scalar1=-1.0, scalar2=-7.0, op0=MULT, op1=ADD
+        )
+        wts = keep.tile([P, 4], F32, name="wts")
+        nc.scalar.activation(out=wts[:], in_=expo[:], func=EXP, scale=0.25)
+        a2s = wts[:, 0:1]
+        a2r = wts[:, 1:2]
+        a0s = wts[:, 2:3]
+        a0r = wts[:, 3:4]
+        cc = keep.tile([P, 8], F32, name="cc")
+        wsum = keep.tile([P, 1], F32, name="wsum")
+        nc.vector.tensor_tensor(out=cc[:, 0:4], in0=consts[:, 4:8], in1=consts[:, 8:12], op=MULT)
+        nc.vector.tensor_tensor(out=wsum[:], in0=a0s, in1=a2s, op=ADD)
+        nc.vector.tensor_scalar_add(out=wsum[:], in0=wsum[:], scalar1=1.0)
+        nc.vector.tensor_scalar_mul(out=cc[:, 4:8], in0=cc[:, 0:4], scalar1=wsum[:])
+
+        wc = keep.tile([P, 12 * P], U32, name="wc", align_bytes=64)
+        wsc = keep.tile([P, 12 * P], U8, name="wsc", align_bytes=64)
+        w_words = w_sb[:].bitcast(F32)
+
+        def prep_w(fb, eng_copy):
+            gw = work.tile([P, 1536], BF16, name="gw", tag="gw", bufs=2, align_bytes=64)
+            gww = gw[:].bitcast(F32).rearrange("p (t o u) -> p t o u", t=3, o=P, u=2)
+            for t0, nt in ((0, 2), (2, 1)):
+                tp = psum.tile([P, 512], F32, name="tpw", tag="tp", bufs=2)
+                for t in range(nt):
+                    for u in range(2):
+                        c0 = (3 * fb + t0 + t) * 256 + u * P
+                        nc.tensor.transpose(
+                            tp[:, (2 * t + u) * P : (2 * t + u + 1) * P], w_words[:, c0 : c0 + P], ident[:]
+                        )
+                eng_copy(
+                    out=gww[:, t0 : t0 + nt],
+                    in_=tp[:, 0 : nt * 256].rearrange("p (t u o) -> p t o u", t=nt, u=2),
+                )
+            for t in range(3):
+                s = (3 * fb + t) * P
+                nc.vector.quantize_mx(
+                    out=wc[:, s : s + P].bitcast(FP8X4),
+                    scales=wsc[:, s : s + P],
+                    in_=gw[:, t * 512 : (t + 1) * 512],
+                )
+
+        prep_w(0, nc.vector.tensor_copy)
+
+        xg = work.tile([P, 8192], F32, name="xg", tag="big", bufs=2)
+        xs_words = xs[:].bitcast(F32).rearrange("p (q j w) -> p q j w", q=64, j=NJ, w=4)
+        xg_view = xg[:].rearrange("p (j q w) -> p j q w", j=NJ, q=64, w=4)
+        for cp in range(4):
+            for jq in range(4):
+                eng_copy = nc.vector.tensor_copy if jq % 2 == 0 else nc.scalar.copy
+                eng_copy(
+                    out=xg_view[:, 8 * jq : 8 * jq + 8, 16 * cp : 16 * cp + 16, :],
+                    in_=xs_words[:, 16 * cp : 16 * cp + 16, 8 * jq : 8 * jq + 8, :].rearrange("p q j w -> p j q w"),
+                )
+        xc = keep.tile([P, 4096], U32, name="xc", align_bytes=64)
+        xsc = keep.tile([P, 4096], U8, name="xsc", align_bytes=64)
+
+        def prep_x(g):
+            gx = work.tile([P, 2048], BF16, name="gx", tag="gx", bufs=3, align_bytes=64)
+            gxw = gx[:].bitcast(F32).rearrange("p (h jj c u) -> p h jj c u", h=2, jj=2, c=P, u=2)
+            for h in range(2):
+                tp = psum.tile([P, 512], F32, name="tpx", tag="tp", bufs=2)
+                for jj in range(2):
+                    for u in range(2):
+                        c0 = (4 * g + 2 * h + jj) * 256 + u * P
+                        nc.tensor.transpose(
+                            tp[:, (2 * jj + u) * P : (2 * jj + u + 1) * P], xg[:, c0 : c0 + P], ident[:]
+                        )
+                nc.scalar.copy(out=gxw[:, h], in_=tp[:].rearrange("p (jj u c) -> p jj c u", jj=2, u=2))
+            nc.vector.quantize_mx(
+                out=xc[:, 512 * g : 512 * g + 512].bitcast(FP8X4),
+                scales=xsc[:, 512 * g : 512 * g + 512],
+                in_=gx[:],
+            )
+
+        def project(dst, slot, g):
+            nc.tensor.matmul_mx(
+                out=dst,
+                lhsT=wc[:, slot * P : (slot + 1) * P].bitcast(FP8X4),
+                lhsT_scale=wsc[:, slot * P : (slot + 1) * P],
+                rhs=xc[:, 512 * g : 512 * g + 512].bitcast(FP8X4),
+                rhs_scale=xsc[:, 512 * g : 512 * g + 512],
+                start=True,
+                stop=True,
+            )
+
+        kv_of = {}
+        hj_of = {}
+        os_of = {}
+
+        def begin_block(fb):
+            kv = work.tile([P, 34 * P], F32, name="kv", tag="kv", bufs=2)
+            hj = work.tile([P, 33 * ROW], F32, name="hj", tag="hj", bufs=2)
+            ost = work.tile([P, 4096], F32, name="ost", tag="big", bufs=2)
+            kv_of[fb] = kv
+            hj_of[fb] = hj
+            os_of[fb] = ost
+            for s in (0, 33):
+                nc.scalar.activation(
+                    out=kv[:, s * P : (s + 1) * P], in_=zero[:, 0:P], func=IDENTITY, bias=cc[:, fb : fb + 1], scale=1.0
+                )
+            nc.scalar.activation(
+                out=hj[:].rearrange("p (j c) -> p j c", c=ROW)[:, :, 0:4],
+                in_=zero[:].rearrange("p (j c) -> p j c", c=4),
+                func=IDENTITY,
+                bias=cc[:, 4 + fb : 5 + fb],
+                scale=1.0,
+            )
+
+        def stage_a(fb, g):
+            kps = psum.tile([P, 512], F32, name="kps", tag="kps", bufs=2)
+            vps = psum.tile([P, 512], F32, name="vps", tag="vps", bufs=2)
+            project(vps[:], 3 * fb + 2, g)
+            project(kps[:], 3 * fb + 1, g)
+            vt = work.tile([P, 512], F32, name="vt", tag="vt", bufs=3)
+            nc.scalar.activation(out=vt[:], in_=vps[:], func=IDENTITY, bias=consts[:, 8 + fb : 9 + fb], scale=1.0)
+            nc.vector.scalar_tensor_tensor(
+                out=kv_of[fb][:, (1 + 4 * g) * P : (5 + 4 * g) * P],
+                in0=kps[:],
+                scalar=consts[:, 4 + fb : 5 + fb],
+                in1=vt[:],
+                op0=ADD,
+                op1=MULT,
+            )
+
+        def stage_b(fb, g):
+            j0 = 4 * g
+            kv = kv_of[fb]
+            hj = hj_of[fb]
+
+            def kwin(s):
+                return kv[:, (j0 + s) * P : (j0 + s + 4) * P].rearrange("p (j c) -> p j c", c=P)
+
+            def hwin(off):
+                return hj[:, off : off + NJ * ROW].rearrange("p (j c) -> p j c", c=ROW)[:, j0 : j0 + 4, 0:P]
+
+            nc.vector.scalar_tensor_tensor(out=hwin(4), in0=kwin(0), scalar=a0s, in1=kwin(1), op0=MULT, op1=ADD)
+            nc.vector.scalar_tensor_tensor(out=hwin(4), in0=kwin(2), scalar=a2s, in1=hwin(4), op0=MULT, op1=ADD)
+            st = work.tile([P, 512], F32, name="st", tag="st", bufs=3)
+            sv = st[:].rearrange("p (j c) -> p j c", c=P)
+            nc.vector.scalar_tensor_tensor(out=sv, in0=hwin(0), scalar=a0r, in1=hwin(4), op0=MULT, op1=ADD)
+            nc.vector.scalar_tensor_tensor(out=sv, in0=hwin(8), scalar=a2r, in1=sv, op0=MULT, op1=ADD)
+            qps = psum.tile([P, 512], F32, name="qps", tag="qps", bufs=2)
+            project(qps[:], 3 * fb, g)
+            nc.vector.scalar_tensor_tensor(
+                out=st[:], in0=qps[:], scalar=consts[:, fb : fb + 1], in1=st[:], op0=ADD, op1=MULT
+            )
+            ot = psum.tile([P, 512], F32, name="ot", tag="tp", bufs=2)
+            for jj in range(4):
+                nc.tensor.transpose(ot[:, jj * P : (jj + 1) * P], st[:, jj * P : (jj + 1) * P], ident[:])
+            nc.scalar.copy(
+                out=os_of[fb][:].rearrange("p (q j s) -> p q j s", q=16, j=NJ, s=8)[:, :, j0 : j0 + 4, :],
+                in_=ot[:].rearrange("p (jj q s) -> p q jj s", jj=4, q=16, s=8),
+            )
+            if g == NG - 1:
+                for b in range(NB):
+                    nc.sync.dma_start(
+                        out=out[b, 2 * fb : 2 * fb + 2].rearrange("c (i r) w -> i c (r w)", r=8),
+                        in_=os_of[fb][b:P:4, :].rearrange("p (c f) -> p c f", c=2),
+                    )
+
+        prep_x(0)
+        prep_x(1)
+        for fb in range(NF):
+            begin_block(fb)
+            for g in range(NG):
+                if fb == 0 and g + 2 < NG:
+                    prep_x(g + 2)
+                if g == 3 and fb + 1 < NF:
+                    prep_w(fb + 1, nc.scalar.copy)
+                stage_a(fb, g)
+                if g >= 1:
+                    stage_b(fb, g - 1)
+            stage_b(fb, NG - 1)

@@ -12,6 +12,7 @@ ADD = mybir.AluOpType.add
 MULT = mybir.AluOpType.mult
 IDENTITY = mybir.ActivationFunctionType.Identity
 EXP = mybir.ActivationFunctionType.Exp
+COPY = mybir.ActivationFunctionType.Copy
 
 FLOPS = 2 * 4096 * 512 * 1536
 
@@ -21,6 +22,7 @@ NJ = 32
 NG = 8
 NF = 4
 ROW = 132
+LAST_STORES = {3: 0, 5: 16, 6: 24, 7: 28}
 
 
 def tile_attentionconv_t_kernel(tc, x, W_qkv, b_qkv, out):
@@ -68,7 +70,8 @@ def tile_attentionconv_t_kernel(tc, x, W_qkv, b_qkv, out):
         nc.tensor.transpose(cps[:, 0:P], zs[:], ident[:])
         nc.tensor.transpose(cps[:, P : 2 * P], zr[:], ident[:])
         bps = psum.tile([P, 512], F32, name="bps", tag="tp", bufs=2)
-        nc.tensor.transpose(bps[:, 0:P], bzf[:], ident[:])
+        nc.tensor.matmul(out=bps[:, 0:P], lhsT=bzf[:], rhs=ident[:], is_transpose=True, start=True, stop=False)
+        nc.tensor.matmul(out=bps[:, 0:P], lhsT=zero[:, 0:P], rhs=ident[:], is_transpose=True, start=False, stop=True)
         consts = keep.tile([P, 12], F32, name="consts")
         nc.vector.tensor_copy(out=consts[:, 0:12], in_=bps[:, 0:12])
         expo = keep.tile([P, 4], F32, name="expo")
@@ -201,7 +204,9 @@ def tile_attentionconv_t_kernel(tc, x, W_qkv, b_qkv, out):
                 op1=MULT,
             )
 
-        def stage_b(fb, g):
+        st_of = {}
+
+        def windows(fb, g):
             j0 = 4 * g
             kv = kv_of[fb]
             hj = hj_of[fb]
@@ -212,11 +217,41 @@ def tile_attentionconv_t_kernel(tc, x, W_qkv, b_qkv, out):
             def hwin(off):
                 return hj[:, off : off + NJ * ROW].rearrange("p (j c) -> p j c", c=ROW)[:, j0 : j0 + 4, 0:P]
 
+            return kwin, hwin
+
+        def stage_b1(fb, g):
+            kwin, hwin = windows(fb, g)
             nc.vector.scalar_tensor_tensor(out=hwin(4), in0=kwin(0), scalar=a0s, in1=kwin(1), op0=MULT, op1=ADD)
             nc.vector.scalar_tensor_tensor(out=hwin(4), in0=kwin(2), scalar=a2s, in1=hwin(4), op0=MULT, op1=ADD)
-            st = work.tile([P, 512], F32, name="st", tag="st", bufs=3)
+            t0 = work.tile([P, 512], F32, name="t0", tag="t0", bufs=2)
+            t0v = t0[:].rearrange("p (j c) -> p j c", c=P)
+            nc.scalar.activation(out=t0v, in_=hwin(0), func=COPY, scale=a0r)
+            st = work.tile([P, 512], F32, name="st", tag="st", bufs=4)
+            st_of[(fb, g)] = st
+            nc.gpsimd.tensor_tensor(out=st[:].rearrange("p (j c) -> p j c", c=P), in0=t0v, in1=hwin(4), op=ADD)
+
+        def store(fb, ja, jb):
+            if ja == 0 and jb == NJ:
+                for b in range(NB):
+                    nc.sync.dma_start(
+                        out=out[b, 2 * fb : 2 * fb + 2].rearrange("c (i r) w -> i c (r w)", r=8),
+                        in_=os_of[fb][b:P:4, :].rearrange("p (c f) -> p c f", c=2),
+                    )
+            else:
+                for b in range(NB):
+                    for c in range(2):
+                        nc.sync.dma_start(
+                            out=out[b, 2 * fb + c].rearrange("(i r) w -> i r w", r=8)[:, :, 8 * ja : 8 * jb],
+                            in_=os_of[fb][b:P:4, c * 2048 : (c + 1) * 2048].rearrange("p (r w) -> p r w", r=8)[
+                                :, :, 8 * ja : 8 * jb
+                            ],
+                        )
+
+        def stage_b2(fb, g):
+            j0 = 4 * g
+            kwin, hwin = windows(fb, g)
+            st = st_of[(fb, g)]
             sv = st[:].rearrange("p (j c) -> p j c", c=P)
-            nc.vector.scalar_tensor_tensor(out=sv, in0=hwin(0), scalar=a0r, in1=hwin(4), op0=MULT, op1=ADD)
             nc.vector.scalar_tensor_tensor(out=sv, in0=hwin(8), scalar=a2r, in1=sv, op0=MULT, op1=ADD)
             qps = psum.tile([P, 512], F32, name="qps", tag="qps", bufs=2)
             project(qps[:], 3 * fb, g)
@@ -230,23 +265,26 @@ def tile_attentionconv_t_kernel(tc, x, W_qkv, b_qkv, out):
                 out=os_of[fb][:].rearrange("p (q j s) -> p q j s", q=16, j=NJ, s=8)[:, :, j0 : j0 + 4, :],
                 in_=ot[:].rearrange("p (jj q s) -> p q jj s", jj=4, q=16, s=8),
             )
-            if g == NG - 1:
-                for b in range(NB):
-                    nc.sync.dma_start(
-                        out=out[b, 2 * fb : 2 * fb + 2].rearrange("c (i r) w -> i c (r w)", r=8),
-                        in_=os_of[fb][b:P:4, :].rearrange("p (c f) -> p c f", c=2),
-                    )
+            if fb < NF - 1:
+                if g == NG - 1:
+                    store(fb, 0, NJ)
+            elif g in LAST_STORES:
+                store(fb, LAST_STORES[g], j0 + 4)
 
         prep_x(0)
         prep_x(1)
-        for fb in range(NF):
-            begin_block(fb)
-            for g in range(NG):
+        units = [(fb, g) for fb in range(NF) for g in range(NG)]
+        for n in range(len(units) + 2):
+            if n < len(units):
+                fb, g = units[n]
+                if g == 0:
+                    begin_block(fb)
                 if fb == 0 and g + 2 < NG:
                     prep_x(g + 2)
                 if g == 3 and fb + 1 < NF:
                     prep_w(fb + 1, nc.scalar.copy)
                 stage_a(fb, g)
-                if g >= 1:
-                    stage_b(fb, g - 1)
-            stage_b(fb, NG - 1)
+            if 1 <= n <= len(units):
+                stage_b1(*units[n - 1])
+            if n >= 2:
+                stage_b2(*units[n - 2])

@@ -66,12 +66,11 @@ def tile_attentionconv_t_kernel(tc, x, W_qkv, b_qkv, out):
 
         bzf = keep.tile([P, P], F32, name="bzf")
         nc.vector.tensor_copy(out=bzf[:], in_=bz[:])
-        cps = psum.tile([P, 512], F32, name="cps", tag="tp", bufs=2)
+        cps = psum.tile([P, 512], F32, name="cps", tag="rot", bufs=4)
         nc.tensor.transpose(cps[:, 0:P], zs[:], ident[:])
         nc.tensor.transpose(cps[:, P : 2 * P], zr[:], ident[:])
-        bps = psum.tile([P, 512], F32, name="bps", tag="tp", bufs=2)
-        nc.tensor.matmul(out=bps[:, 0:P], lhsT=bzf[:], rhs=ident[:], is_transpose=True, start=True, stop=False)
-        nc.tensor.matmul(out=bps[:, 0:P], lhsT=zero[:, 0:P], rhs=ident[:], is_transpose=True, start=False, stop=True)
+        bps = psum.tile([P, 512], F32, name="bps", tag="rot", bufs=4)
+        nc.tensor.transpose(bps[:, 0:P], bzf[:], ident[:])
         consts = keep.tile([P, 12], F32, name="consts")
         nc.vector.tensor_copy(out=consts[:, 0:12], in_=bps[:, 0:12])
         expo = keep.tile([P, 4], F32, name="expo")
@@ -102,7 +101,7 @@ def tile_attentionconv_t_kernel(tc, x, W_qkv, b_qkv, out):
             gw = work.tile([P, 1536], BF16, name="gw", tag="gw", bufs=2, align_bytes=64)
             gww = gw[:].bitcast(F32).rearrange("p (t o u) -> p t o u", t=3, o=P, u=2)
             for t0, nt in ((0, 2), (2, 1)):
-                tp = psum.tile([P, 512], F32, name="tpw", tag="tp", bufs=2)
+                tp = psum.tile([P, 512], F32, name="tpw", tag="rot", bufs=4)
                 for t in range(nt):
                     for u in range(2):
                         c0 = (3 * fb + t0 + t) * 256 + u * P
@@ -140,7 +139,7 @@ def tile_attentionconv_t_kernel(tc, x, W_qkv, b_qkv, out):
             gx = work.tile([P, 2048], BF16, name="gx", tag="gx", bufs=3, align_bytes=64)
             gxw = gx[:].bitcast(F32).rearrange("p (h jj c u) -> p h jj c u", h=2, jj=2, c=P, u=2)
             for h in range(2):
-                tp = psum.tile([P, 512], F32, name="tpx", tag="tp", bufs=2)
+                tp = psum.tile([P, 512], F32, name="tpx", tag="rot", bufs=4)
                 for jj in range(2):
                     for u in range(2):
                         c0 = (4 * g + 2 * h + jj) * 256 + u * P
@@ -188,13 +187,20 @@ def tile_attentionconv_t_kernel(tc, x, W_qkv, b_qkv, out):
                 scale=1.0,
             )
 
+        qt_of = {}
+        st_of = {}
+
         def stage_a(fb, g):
             kps = psum.tile([P, 512], F32, name="kps", tag="kps", bufs=2)
             vps = psum.tile([P, 512], F32, name="vps", tag="vps", bufs=2)
+            qps = psum.tile([P, 512], F32, name="qps", tag="rot", bufs=4)
             project(vps[:], 3 * fb + 2, g)
             project(kps[:], 3 * fb + 1, g)
+            project(qps[:], 3 * fb, g)
             vt = work.tile([P, 512], F32, name="vt", tag="vt", bufs=3)
             nc.scalar.activation(out=vt[:], in_=vps[:], func=IDENTITY, bias=consts[:, 8 + fb : 9 + fb], scale=1.0)
+            qs = work.tile([P, 512], F32, name="qs", tag="qs", bufs=2)
+            nc.scalar.activation(out=qs[:], in_=qps[:], func=IDENTITY, bias=consts[:, fb : fb + 1], scale=1.0)
             nc.vector.scalar_tensor_tensor(
                 out=kv_of[fb][:, (1 + 4 * g) * P : (5 + 4 * g) * P],
                 in0=kps[:],
@@ -203,10 +209,17 @@ def tile_attentionconv_t_kernel(tc, x, W_qkv, b_qkv, out):
                 op0=ADD,
                 op1=MULT,
             )
+            qtp = psum.tile([P, 512], F32, name="qtp", tag="rot", bufs=4)
+            for jj in range(4):
+                nc.tensor.transpose(qtp[:, jj * P : (jj + 1) * P], qs[:, jj * P : (jj + 1) * P], ident[:])
+            qts = work.tile([P, 512], F32, name="qts", tag="qts", bufs=4)
+            qt_of[(fb, g)] = qts
+            nc.scalar.copy(
+                out=qts[:].rearrange("p (q jj s) -> p q jj s", q=16, jj=4, s=8),
+                in_=qtp[:].rearrange("p (jj q s) -> p q jj s", jj=4, q=16, s=8),
+            )
 
-        st_of = {}
-
-        def windows(fb, g):
+        def stage_b(fb, g):
             j0 = 4 * g
             kv = kv_of[fb]
             hj = hj_of[fb]
@@ -217,18 +230,24 @@ def tile_attentionconv_t_kernel(tc, x, W_qkv, b_qkv, out):
             def hwin(off):
                 return hj[:, off : off + NJ * ROW].rearrange("p (j c) -> p j c", c=ROW)[:, j0 : j0 + 4, 0:P]
 
-            return kwin, hwin
-
-        def stage_b1(fb, g):
-            kwin, hwin = windows(fb, g)
             nc.vector.scalar_tensor_tensor(out=hwin(4), in0=kwin(0), scalar=a0s, in1=kwin(1), op0=MULT, op1=ADD)
             nc.vector.scalar_tensor_tensor(out=hwin(4), in0=kwin(2), scalar=a2s, in1=hwin(4), op0=MULT, op1=ADD)
-            t0 = work.tile([P, 512], F32, name="t0", tag="t0", bufs=2)
-            t0v = t0[:].rearrange("p (j c) -> p j c", c=P)
-            nc.scalar.activation(out=t0v, in_=hwin(0), func=COPY, scale=a0r)
-            st = work.tile([P, 512], F32, name="st", tag="st", bufs=4)
-            st_of[(fb, g)] = st
-            nc.gpsimd.tensor_tensor(out=st[:].rearrange("p (j c) -> p j c", c=P), in0=t0v, in1=hwin(4), op=ADD)
+            t0 = work.tile([P, 512], F32, name="t0", tag="t0", bufs=3)
+            t2 = work.tile([P, 512], F32, name="t2", tag="t2", bufs=3)
+            nc.scalar.activation(out=t0[:].rearrange("p (j c) -> p j c", c=P), in_=hwin(0), func=COPY, scale=a0r)
+            nc.vector.tensor_scalar_mul(out=t2[:].rearrange("p (j c) -> p j c", c=P), in0=hwin(8), scalar1=a2r)
+            stp = psum.tile([P, 512], F32, name="stp", tag="rot", bufs=4)
+            st_of[(fb, g)] = stp
+            for jj in range(4):
+                dst = stp[:, jj * P : (jj + 1) * P]
+                c0 = (j0 + jj) * ROW + 4
+                nc.tensor.matmul(out=dst, lhsT=hj[:, c0 : c0 + P], rhs=ident[:], is_transpose=True, start=True, stop=False)
+                nc.tensor.matmul(
+                    out=dst, lhsT=t0[:, jj * P : (jj + 1) * P], rhs=ident[:], is_transpose=True, start=False, stop=False
+                )
+                nc.tensor.matmul(
+                    out=dst, lhsT=t2[:, jj * P : (jj + 1) * P], rhs=ident[:], is_transpose=True, start=False, stop=True
+                )
 
         def store(fb, ja, jb):
             if ja == 0 and jb == NJ:
@@ -247,23 +266,13 @@ def tile_attentionconv_t_kernel(tc, x, W_qkv, b_qkv, out):
                             ],
                         )
 
-        def stage_b2(fb, g):
+        def stage_f(fb, g):
             j0 = 4 * g
-            kwin, hwin = windows(fb, g)
-            st = st_of[(fb, g)]
-            sv = st[:].rearrange("p (j c) -> p j c", c=P)
-            nc.vector.scalar_tensor_tensor(out=sv, in0=hwin(8), scalar=a2r, in1=sv, op0=MULT, op1=ADD)
-            qps = psum.tile([P, 512], F32, name="qps", tag="qps", bufs=2)
-            project(qps[:], 3 * fb, g)
-            nc.vector.scalar_tensor_tensor(
-                out=st[:], in0=qps[:], scalar=consts[:, fb : fb + 1], in1=st[:], op0=ADD, op1=MULT
-            )
-            ot = psum.tile([P, 512], F32, name="ot", tag="tp", bufs=2)
-            for jj in range(4):
-                nc.tensor.transpose(ot[:, jj * P : (jj + 1) * P], st[:, jj * P : (jj + 1) * P], ident[:])
-            nc.scalar.copy(
+            nc.vector.tensor_tensor(
                 out=os_of[fb][:].rearrange("p (q j s) -> p q j s", q=16, j=NJ, s=8)[:, :, j0 : j0 + 4, :],
-                in_=ot[:].rearrange("p (jj q s) -> p q jj s", jj=4, q=16, s=8),
+                in0=st_of[(fb, g)][:].rearrange("p (jj q s) -> p q jj s", jj=4, q=16, s=8),
+                in1=qt_of[(fb, g)][:].rearrange("p (q jj s) -> p q jj s", q=16, jj=4, s=8),
+                op=MULT,
             )
             if fb < NF - 1:
                 if g == NG - 1:
@@ -285,6 +294,6 @@ def tile_attentionconv_t_kernel(tc, x, W_qkv, b_qkv, out):
                     prep_w(fb + 1, nc.scalar.copy)
                 stage_a(fb, g)
             if 1 <= n <= len(units):
-                stage_b1(*units[n - 1])
+                stage_b(*units[n - 1])
             if n >= 2:
-                stage_b2(*units[n - 2])
+                stage_f(*units[n - 2])

@@ -31,6 +31,7 @@ def tile_attentionconv_t_kernel(tc, x, W_qkv, b_qkv, out):
         keep = ctx.enter_context(tc.tile_pool(name="keep", bufs=1))
         work = ctx.enter_context(tc.tile_pool(name="work", bufs=2))
         psum = ctx.enter_context(tc.psum_pool(name="psum", bufs=2))
+        ctx.enter_context(tc.manual_schedule())
 
         ident = keep.tile([P, P], F32, name="ident")
         make_identity(nc, ident[:])
@@ -66,10 +67,10 @@ def tile_attentionconv_t_kernel(tc, x, W_qkv, b_qkv, out):
 
         bzf = keep.tile([P, P], F32, name="bzf")
         nc.vector.tensor_copy(out=bzf[:], in_=bz[:])
-        cps = psum.tile([P, 512], F32, name="cps", tag="rot", bufs=4)
+        cps = psum.tile([P, 512], F32, name="cps", tag="tp", bufs=2)
         nc.tensor.transpose(cps[:, 0:P], zs[:], ident[:])
         nc.tensor.transpose(cps[:, P : 2 * P], zr[:], ident[:])
-        bps = psum.tile([P, 512], F32, name="bps", tag="rot", bufs=4)
+        bps = psum.tile([P, 512], F32, name="bps", tag="tp", bufs=2)
         nc.tensor.transpose(bps[:, 0:P], bzf[:], ident[:])
         consts = keep.tile([P, 12], F32, name="consts")
         nc.vector.tensor_copy(out=consts[:, 0:12], in_=bps[:, 0:12])
@@ -97,11 +98,14 @@ def tile_attentionconv_t_kernel(tc, x, W_qkv, b_qkv, out):
         wsc = keep.tile([P, 12 * P], U8, name="wsc", align_bytes=64)
         w_words = w_sb[:].bitcast(F32)
 
-        def prep_w(fb, eng_copy):
+        gw_of = {}
+
+        def w_transpose(fb, eng_copy):
             gw = work.tile([P, 1536], BF16, name="gw", tag="gw", bufs=2, align_bytes=64)
+            gw_of[fb] = gw
             gww = gw[:].bitcast(F32).rearrange("p (t o u) -> p t o u", t=3, o=P, u=2)
             for t0, nt in ((0, 2), (2, 1)):
-                tp = psum.tile([P, 512], F32, name="tpw", tag="rot", bufs=4)
+                tp = psum.tile([P, 512], F32, name="tpw", tag="tp", bufs=2)
                 for t in range(nt):
                     for u in range(2):
                         c0 = (3 * fb + t0 + t) * 256 + u * P
@@ -112,6 +116,9 @@ def tile_attentionconv_t_kernel(tc, x, W_qkv, b_qkv, out):
                     out=gww[:, t0 : t0 + nt],
                     in_=tp[:, 0 : nt * 256].rearrange("p (t u o) -> p t o u", t=nt, u=2),
                 )
+
+        def w_quantise(fb):
+            gw = gw_of[fb]
             for t in range(3):
                 s = (3 * fb + t) * P
                 nc.vector.quantize_mx(
@@ -120,7 +127,8 @@ def tile_attentionconv_t_kernel(tc, x, W_qkv, b_qkv, out):
                     in_=gw[:, t * 512 : (t + 1) * 512],
                 )
 
-        prep_w(0, nc.vector.tensor_copy)
+        w_transpose(0, nc.vector.tensor_copy)
+        w_quantise(0)
 
         xg = work.tile([P, 8192], F32, name="xg", tag="big", bufs=2)
         xs_words = xs[:].bitcast(F32).rearrange("p (q j w) -> p q j w", q=64, j=NJ, w=4)
@@ -135,22 +143,34 @@ def tile_attentionconv_t_kernel(tc, x, W_qkv, b_qkv, out):
         xc = keep.tile([P, 4096], U32, name="xc", align_bytes=64)
         xsc = keep.tile([P, 4096], U8, name="xsc", align_bytes=64)
 
-        def prep_x(g):
-            gx = work.tile([P, 2048], BF16, name="gx", tag="gx", bufs=3, align_bytes=64)
-            gxw = gx[:].bitcast(F32).rearrange("p (h jj c u) -> p h jj c u", h=2, jj=2, c=P, u=2)
+        gx_of = {}
+        tpx_of = {}
+
+        def x_transpose(g):
             for h in range(2):
-                tp = psum.tile([P, 512], F32, name="tpx", tag="rot", bufs=4)
+                tp = psum.tile([P, 512], F32, name="tpx", tag="tp", bufs=2)
+                tpx_of[(g, h)] = tp
                 for jj in range(2):
                     for u in range(2):
                         c0 = (4 * g + 2 * h + jj) * 256 + u * P
                         nc.tensor.transpose(
                             tp[:, (2 * jj + u) * P : (2 * jj + u + 1) * P], xg[:, c0 : c0 + P], ident[:]
                         )
-                nc.scalar.copy(out=gxw[:, h], in_=tp[:].rearrange("p (jj u c) -> p jj c u", jj=2, u=2))
+
+        def x_copy(g):
+            gx = work.tile([P, 2048], BF16, name="gx", tag="gx", bufs=3, align_bytes=64)
+            gx_of[g] = gx
+            gxw = gx[:].bitcast(F32).rearrange("p (h jj c u) -> p h jj c u", h=2, jj=2, c=P, u=2)
+            for h in range(2):
+                nc.scalar.copy(
+                    out=gxw[:, h], in_=tpx_of[(g, h)][:].rearrange("p (jj u c) -> p jj c u", jj=2, u=2)
+                )
+
+        def x_quantise(g):
             nc.vector.quantize_mx(
                 out=xc[:, 512 * g : 512 * g + 512].bitcast(FP8X4),
                 scales=xsc[:, 512 * g : 512 * g + 512],
-                in_=gx[:],
+                in_=gx_of[g][:],
             )
 
         def project(dst, slot, g):
@@ -187,61 +207,99 @@ def tile_attentionconv_t_kernel(tc, x, W_qkv, b_qkv, out):
                 scale=1.0,
             )
 
-        qt_of = {}
-        st_of = {}
+        units = [(fb, g) for fb in range(NF) for g in range(NG)]
+        n_units = len(units)
+        tiles = {}
 
-        def stage_a(fb, g):
-            kps = psum.tile([P, 512], F32, name="kps", tag="kps", bufs=2)
-            vps = psum.tile([P, 512], F32, name="vps", tag="vps", bufs=2)
-            qps = psum.tile([P, 512], F32, name="qps", tag="rot", bufs=4)
+        def hwin(u, off):
+            fb, g = units[u]
+            return hj_of[fb][:, off : off + NJ * ROW].rearrange("p (j c) -> p j c", c=ROW)[:, 4 * g : 4 * g + 4, 0:P]
+
+        def kwin(u, s):
+            fb, g = units[u]
+            return kv_of[fb][:, (4 * g + s) * P : (4 * g + s + 4) * P].rearrange("p (j c) -> p j c", c=P)
+
+        def pe_project(u):
+            fb, g = units[u]
+            vps = psum.tile([P, 512], F32, name="vps", tag="vps", bufs=1)
+            kps = psum.tile([P, 512], F32, name="kps", tag="kps", bufs=1)
+            qps = psum.tile([P, 512], F32, name="qps", tag="qps", bufs=1)
+            tiles[("v", u)] = vps
+            tiles[("k", u)] = kps
+            tiles[("q", u)] = qps
             project(vps[:], 3 * fb + 2, g)
             project(kps[:], 3 * fb + 1, g)
             project(qps[:], 3 * fb, g)
-            vt = work.tile([P, 512], F32, name="vt", tag="vt", bufs=3)
-            nc.scalar.activation(out=vt[:], in_=vps[:], func=IDENTITY, bias=consts[:, 8 + fb : 9 + fb], scale=1.0)
+
+        def act_v_q(u):
+            fb, g = units[u]
+            vt = work.tile([P, 512], F32, name="vt", tag="vt", bufs=2)
             qs = work.tile([P, 512], F32, name="qs", tag="qs", bufs=2)
-            nc.scalar.activation(out=qs[:], in_=qps[:], func=IDENTITY, bias=consts[:, fb : fb + 1], scale=1.0)
+            tiles[("vt", u)] = vt
+            tiles[("qs", u)] = qs
+            nc.scalar.activation(
+                out=vt[:], in_=tiles[("v", u)][:], func=IDENTITY, bias=consts[:, 8 + fb : 9 + fb], scale=1.0
+            )
+            nc.scalar.activation(
+                out=qs[:], in_=tiles[("q", u)][:], func=IDENTITY, bias=consts[:, fb : fb + 1], scale=1.0
+            )
+
+        def dve_kv(u):
+            fb, g = units[u]
             nc.vector.scalar_tensor_tensor(
                 out=kv_of[fb][:, (1 + 4 * g) * P : (5 + 4 * g) * P],
-                in0=kps[:],
+                in0=tiles[("k", u)][:],
                 scalar=consts[:, 4 + fb : 5 + fb],
-                in1=vt[:],
+                in1=tiles[("vt", u)][:],
                 op0=ADD,
                 op1=MULT,
             )
-            qtp = psum.tile([P, 512], F32, name="qtp", tag="rot", bufs=4)
+
+        def pe_q_transpose(u):
+            qtp = psum.tile([P, 512], F32, name="qtp", tag="qtp", bufs=1)
+            tiles[("qtp", u)] = qtp
+            qs = tiles[("qs", u)]
             for jj in range(4):
                 nc.tensor.transpose(qtp[:, jj * P : (jj + 1) * P], qs[:, jj * P : (jj + 1) * P], ident[:])
-            qts = work.tile([P, 512], F32, name="qts", tag="qts", bufs=4)
-            qt_of[(fb, g)] = qts
+
+        def act_q_copy(u):
+            qts = work.tile([P, 512], F32, name="qts", tag="qts", bufs=6)
+            tiles[("qts", u)] = qts
             nc.scalar.copy(
                 out=qts[:].rearrange("p (q jj s) -> p q jj s", q=16, jj=4, s=8),
-                in_=qtp[:].rearrange("p (jj q s) -> p q jj s", jj=4, q=16, s=8),
+                in_=tiles[("qtp", u)][:].rearrange("p (jj q s) -> p q jj s", jj=4, q=16, s=8),
             )
 
-        def stage_b(fb, g):
-            j0 = 4 * g
-            kv = kv_of[fb]
-            hj = hj_of[fb]
+        def dve_columns(u):
+            nc.vector.scalar_tensor_tensor(
+                out=hwin(u, 4), in0=kwin(u, 0), scalar=a0s, in1=kwin(u, 1), op0=MULT, op1=ADD
+            )
+            nc.vector.scalar_tensor_tensor(
+                out=hwin(u, 4), in0=kwin(u, 2), scalar=a2s, in1=hwin(u, 4), op0=MULT, op1=ADD
+            )
 
-            def kwin(s):
-                return kv[:, (j0 + s) * P : (j0 + s + 4) * P].rearrange("p (j c) -> p j c", c=P)
-
-            def hwin(off):
-                return hj[:, off : off + NJ * ROW].rearrange("p (j c) -> p j c", c=ROW)[:, j0 : j0 + 4, 0:P]
-
-            nc.vector.scalar_tensor_tensor(out=hwin(4), in0=kwin(0), scalar=a0s, in1=kwin(1), op0=MULT, op1=ADD)
-            nc.vector.scalar_tensor_tensor(out=hwin(4), in0=kwin(2), scalar=a2s, in1=hwin(4), op0=MULT, op1=ADD)
+        def act_scale_up(u):
             t0 = work.tile([P, 512], F32, name="t0", tag="t0", bufs=3)
+            tiles[("t0", u)] = t0
+            nc.scalar.activation(out=t0[:].rearrange("p (j c) -> p j c", c=P), in_=hwin(u, 0), func=COPY, scale=a0r)
+
+        def dve_scale_down(u):
             t2 = work.tile([P, 512], F32, name="t2", tag="t2", bufs=3)
-            nc.scalar.activation(out=t0[:].rearrange("p (j c) -> p j c", c=P), in_=hwin(0), func=COPY, scale=a0r)
-            nc.vector.tensor_scalar_mul(out=t2[:].rearrange("p (j c) -> p j c", c=P), in0=hwin(8), scalar1=a2r)
-            stp = psum.tile([P, 512], F32, name="stp", tag="rot", bufs=4)
-            st_of[(fb, g)] = stp
+            tiles[("t2", u)] = t2
+            nc.vector.tensor_scalar_mul(out=t2[:].rearrange("p (j c) -> p j c", c=P), in0=hwin(u, 8), scalar1=a2r)
+
+        def pe_rows(u):
+            fb, g = units[u]
+            stp = psum.tile([P, 512], F32, name="stp", tag="stp", bufs=2)
+            tiles[("stp", u)] = stp
+            t0 = tiles[("t0", u)]
+            t2 = tiles[("t2", u)]
             for jj in range(4):
                 dst = stp[:, jj * P : (jj + 1) * P]
-                c0 = (j0 + jj) * ROW + 4
-                nc.tensor.matmul(out=dst, lhsT=hj[:, c0 : c0 + P], rhs=ident[:], is_transpose=True, start=True, stop=False)
+                c0 = (4 * g + jj) * ROW + 4
+                nc.tensor.matmul(
+                    out=dst, lhsT=hj_of[fb][:, c0 : c0 + P], rhs=ident[:], is_transpose=True, start=True, stop=False
+                )
                 nc.tensor.matmul(
                     out=dst, lhsT=t0[:, jj * P : (jj + 1) * P], rhs=ident[:], is_transpose=True, start=False, stop=False
                 )
@@ -266,12 +324,13 @@ def tile_attentionconv_t_kernel(tc, x, W_qkv, b_qkv, out):
                             ],
                         )
 
-        def stage_f(fb, g):
+        def dve_final(u):
+            fb, g = units[u]
             j0 = 4 * g
             nc.vector.tensor_tensor(
                 out=os_of[fb][:].rearrange("p (q j s) -> p q j s", q=16, j=NJ, s=8)[:, :, j0 : j0 + 4, :],
-                in0=st_of[(fb, g)][:].rearrange("p (jj q s) -> p q jj s", jj=4, q=16, s=8),
-                in1=qt_of[(fb, g)][:].rearrange("p (q jj s) -> p q jj s", q=16, jj=4, s=8),
+                in0=tiles[("stp", u)][:].rearrange("p (jj q s) -> p q jj s", jj=4, q=16, s=8),
+                in1=tiles[("qts", u)][:].rearrange("p (q jj s) -> p q jj s", q=16, jj=4, s=8),
                 op=MULT,
             )
             if fb < NF - 1:
@@ -280,20 +339,44 @@ def tile_attentionconv_t_kernel(tc, x, W_qkv, b_qkv, out):
             elif g in LAST_STORES:
                 store(fb, LAST_STORES[g], j0 + 4)
 
-        prep_x(0)
-        prep_x(1)
-        units = [(fb, g) for fb in range(NF) for g in range(NG)]
-        for n in range(len(units) + 2):
-            if n < len(units):
-                fb, g = units[n]
-                if g == 0:
-                    begin_block(fb)
-                if fb == 0 and g + 2 < NG:
-                    prep_x(g + 2)
-                if g == 3 and fb + 1 < NF:
-                    prep_w(fb + 1, nc.scalar.copy)
-                stage_a(fb, g)
-            if 1 <= n <= len(units):
-                stage_b(*units[n - 1])
-            if n >= 2:
-                stage_f(*units[n - 2])
+        def live(u):
+            return 0 <= u < n_units
+
+        for g in range(3):
+            x_transpose(g)
+            x_copy(g)
+            if g >= 1:
+                x_quantise(g - 1)
+        for s in range(-1, n_units + 3):
+            if live(s - 1):
+                dve_scale_down(s - 1)
+            if live(s + 1):
+                if units[s + 1][1] == 0:
+                    begin_block(units[s + 1][0])
+                pe_project(s + 1)
+            if live(s - 3):
+                dve_final(s - 3)
+            if live(s + 1):
+                act_v_q(s + 1)
+            if live(s - 2):
+                pe_rows(s - 2)
+            if live(s + 1):
+                dve_kv(s + 1)
+            if live(s - 1):
+                act_scale_up(s - 1)
+            if live(s + 1):
+                pe_q_transpose(s + 1)
+            if 0 <= s + 3 < NG and s + 3 >= 3:
+                x_transpose(s + 3)
+            if live(s):
+                dve_columns(s)
+            if 0 <= s + 2 < NG and s + 2 >= 2:
+                x_quantise(s + 2)
+            if live(s) and units[s][1] == 5 and units[s][0] + 1 < NF:
+                w_quantise(units[s][0] + 1)
+            if live(s + 1):
+                act_q_copy(s + 1)
+            if 0 <= s + 3 < NG and s + 3 >= 3:
+                x_copy(s + 3)
+            if live(s) and units[s][1] == 3 and units[s][0] + 1 < NF:
+                w_transpose(units[s][0] + 1, nc.scalar.copy)

from contextlib import ExitStack

import concourse.mybir as mybir
from concourse.masks import make_identity

F32 = mybir.dt.float32
BF16 = mybir.dt.bfloat16
U32 = mybir.dt.uint32
U8 = mybir.dt.uint8
FP8X4 = mybir.dt.float8_e4m3fn_x4
ADD = mybir.AluOpType.add
MULT = mybir.AluOpType.mult
IDENTITY = mybir.ActivationFunctionType.Identity
EXP = mybir.ActivationFunctionType.Exp
COPY = mybir.ActivationFunctionType.Copy

FLOPS = 2 * 4096 * 512 * 1536

P = 128
NB = 4
NJ = 32
NG = 8
NF = 4
ROW = 132
LAST_STORES = {3: 0, 5: 16, 6: 24, 7: 28}


def tile_attentionconv_t_kernel(tc, x, W_qkv, b_qkv, out):
    nc = tc.nc
    with ExitStack() as ctx:
        keep = ctx.enter_context(tc.tile_pool(name="keep", bufs=1))
        work = ctx.enter_context(tc.tile_pool(name="work", bufs=2))
        psum = ctx.enter_context(tc.psum_pool(name="psum", bufs=2))
        ctx.enter_context(tc.manual_schedule())

        ident = keep.tile([P, P], F32, name="ident")
        make_identity(nc, ident[:])
        zero = keep.tile([P, ROW], F32, name="zero")
        nc.vector.memset(zero[:], 0.0)
        zs = keep.tile([P, P], F32, name="zs")
        zr = keep.tile([P, P], F32, name="zr")
        for t in range(8):
            nc.vector.memset(zs[:].rearrange("p (a s) -> p a s", s=8)[:, :, t : t + 1], float(-t))
            nc.gpsimd.memset(zr[:].rearrange("p (c r s) -> p c r s", c=2, r=8)[:, :, t : t + 1, :], float(-t))
        bz = keep.tile([P, P], BF16, name="bz")
        nc.vector.memset(bz[:], 0.0)
        nc.sync.dma_start(out=bz[0:12, :], in_=b_qkv.rearrange("(s p) -> s p", p=P))

        w_sb = keep.tile([P, 12 * 512], BF16, name="w_sb")
        w_view = W_qkv.rearrange("(t f p) e -> f p t e", t=3, f=NF, p=P)

        def load_w(fb):
            nc.sync.dma_start(
                out=w_sb[:, fb * 1536 : (fb + 1) * 1536].rearrange("p (t e) -> p t e", t=3), in_=w_view[fb]
            )

        load_w(0)
        xs = work.tile([P, 16384], BF16, name="xs", tag="big", bufs=2)
        for cp in range(4):
            for b in range(NB):
                nc.sync.dma_start(
                    out=xs[b:P:4, cp * 4096 : (cp + 1) * 4096].rearrange("p (c f) -> p c f", c=2),
                    in_=x[b, 2 * cp : 2 * cp + 2].rearrange("c (i r) w -> i c (r w)", r=8),
                )
        for fb in range(1, NF):
            load_w(fb)

        bzf = keep.tile([P, P], F32, name="bzf")
        nc.vector.tensor_copy(out=bzf[:], in_=bz[:])
        cps = psum.tile([P, 512], F32, name="cps", tag="tp", bufs=2)
        nc.tensor.transpose(cps[:, 0:P], zs[:], ident[:])
        nc.tensor.transpose(cps[:, P : 2 * P], zr[:], ident[:])
        bps = psum.tile([P, 512], F32, name="bps", tag="tp", bufs=2)
        nc.tensor.transpose(bps[:, 0:P], bzf[:], ident[:])
        consts = keep.tile([P, 12], F32, name="consts")
        nc.vector.tensor_copy(out=consts[:, 0:12], in_=bps[:, 0:12])
        expo = keep.tile([P, 4], F32, name="expo")
        nc.vector.tensor_copy(
            out=expo[:, 0:2].unsqueeze(2), in_=cps[:, 0 : 2 * P].rearrange("p (w c) -> p w c", c=P)[:, :, 0:1]
        )
        nc.vector.tensor_scalar(
            out=expo[:, 2:4], in0=expo[:, 0:2], scalar1=-1.0, scalar2=-7.0, op0=MULT, op1=ADD
        )
        wts = keep.tile([P, 4], F32, name="wts")
        nc.scalar.activation(out=wts[:], in_=expo[:], func=EXP, scale=0.25)
        a2s = wts[:, 0:1]
        a2r = wts[:, 1:2]
        a0s = wts[:, 2:3]
        a0r = wts[:, 3:4]
        cc = keep.tile([P, 8], F32, name="cc")
        wsum = keep.tile([P, 1], F32, name="wsum")
        nc.vector.tensor_tensor(out=cc[:, 0:4], in0=consts[:, 4:8], in1=consts[:, 8:12], op=MULT)
        nc.vector.tensor_tensor(out=wsum[:], in0=a0s, in1=a2s, op=ADD)
        nc.vector.tensor_scalar_add(out=wsum[:], in0=wsum[:], scalar1=1.0)
        nc.vector.tensor_scalar_mul(out=cc[:, 4:8], in0=cc[:, 0:4], scalar1=wsum[:])

        wc = keep.tile([P, 12 * P], U32, name="wc", align_bytes=64)
        wsc = keep.tile([P, 12 * P], U8, name="wsc", align_bytes=64)
        w_words = w_sb[:].bitcast(F32)

        gw_of = {}

        def w_transpose(fb, eng_copy):
            gw = work.tile([P, 1536], BF16, name="gw", tag="gw", bufs=2, align_bytes=64)
            gw_of[fb] = gw
            gww = gw[:].bitcast(F32).rearrange("p (t o u) -> p t o u", t=3, o=P, u=2)
            for t0, nt in ((0, 2), (2, 1)):
                tp = psum.tile([P, 512], F32, name="tpw", tag="tp", bufs=2)
                for t in range(nt):
                    for u in range(2):
                        c0 = (3 * fb + t0 + t) * 256 + u * P
                        nc.tensor.transpose(
                            tp[:, (2 * t + u) * P : (2 * t + u + 1) * P], w_words[:, c0 : c0 + P], ident[:]
                        )
                eng_copy(
                    out=gww[:, t0 : t0 + nt],
                    in_=tp[:, 0 : nt * 256].rearrange("p (t u o) -> p t o u", t=nt, u=2),
                )

        def w_quantise(fb):
            gw = gw_of[fb]
            for t in range(3):
                s = (3 * fb + t) * P
                nc.vector.quantize_mx(
                    out=wc[:, s : s + P].bitcast(FP8X4),
                    scales=wsc[:, s : s + P],
                    in_=gw[:, t * 512 : (t + 1) * 512],
                )

        w_transpose(0, nc.vector.tensor_copy)
        w_quantise(0)

        xg = work.tile([P, 8192], F32, name="xg", tag="big", bufs=2)
        xs_words = xs[:].bitcast(F32).rearrange("p (q j w) -> p q j w", q=64, j=NJ, w=4)
        xg_view = xg[:].rearrange("p (j q w) -> p j q w", j=NJ, q=64, w=4)
        for cp in range(4):
            for jq in range(4):
                eng_copy = nc.vector.tensor_copy if jq % 2 == 0 else nc.scalar.copy
                eng_copy(
                    out=xg_view[:, 8 * jq : 8 * jq + 8, 16 * cp : 16 * cp + 16, :],
                    in_=xs_words[:, 16 * cp : 16 * cp + 16, 8 * jq : 8 * jq + 8, :].rearrange("p q j w -> p j q w"),
                )
        xc = keep.tile([P, 4096], U32, name="xc", align_bytes=64)
        xsc = keep.tile([P, 4096], U8, name="xsc", align_bytes=64)

        gx_of = {}
        tpx_of = {}

        def x_transpose(g):
            for h in range(2):
                tp = psum.tile([P, 512], F32, name="tpx", tag="tp", bufs=2)
                tpx_of[(g, h)] = tp
                for jj in range(2):
                    for u in range(2):
                        c0 = (4 * g + 2 * h + jj) * 256 + u * P
                        nc.tensor.transpose(
                            tp[:, (2 * jj + u) * P : (2 * jj + u + 1) * P], xg[:, c0 : c0 + P], ident[:]
                        )

        def x_copy(g):
            gx = work.tile([P, 2048], BF16, name="gx", tag="gx", bufs=3, align_bytes=64)
            gx_of[g] = gx
            gxw = gx[:].bitcast(F32).rearrange("p (h jj c u) -> p h jj c u", h=2, jj=2, c=P, u=2)
            for h in range(2):
                nc.scalar.copy(
                    out=gxw[:, h], in_=tpx_of[(g, h)][:].rearrange("p (jj u c) -> p jj c u", jj=2, u=2)
                )

        def x_quantise(g):
            nc.vector.quantize_mx(
                out=xc[:, 512 * g : 512 * g + 512].bitcast(FP8X4),
                scales=xsc[:, 512 * g : 512 * g + 512],
                in_=gx_of[g][:],
            )

        def project(dst, slot, g):
            nc.tensor.matmul_mx(
                out=dst,
                lhsT=wc[:, slot * P : (slot + 1) * P].bitcast(FP8X4),
                lhsT_scale=wsc[:, slot * P : (slot + 1) * P],
                rhs=xc[:, 512 * g : 512 * g + 512].bitcast(FP8X4),
                rhs_scale=xsc[:, 512 * g : 512 * g + 512],
                start=True,
                stop=True,
            )

        kv_of = {}
        hj_of = {}
        os_of = {}

        def begin_block(fb):
            kv = work.tile([P, 34 * P], F32, name="kv", tag="kv", bufs=2)
            hj = work.tile([P, 33 * ROW], F32, name="hj", tag="hj", bufs=2)
            ost = work.tile([P, 4096], F32, name="ost", tag="big", bufs=2)
            kv_of[fb] = kv
            hj_of[fb] = hj
            os_of[fb] = ost
            for s in (0, 33):
                nc.scalar.activation(
                    out=kv[:, s * P : (s + 1) * P], in_=zero[:, 0:P], func=IDENTITY, bias=cc[:, fb : fb + 1], scale=1.0
                )
            nc.scalar.activation(
                out=hj[:].rearrange("p (j c) -> p j c", c=ROW)[:, :, 0:4],
                in_=zero[:].rearrange("p (j c) -> p j c", c=4),
                func=IDENTITY,
                bias=cc[:, 4 + fb : 5 + fb],
                scale=1.0,
            )

        units = [(fb, g) for fb in range(NF) for g in range(NG)]
        n_units = len(units)
        tiles = {}

        def hwin(u, off):
            fb, g = units[u]
            return hj_of[fb][:, off : off + NJ * ROW].rearrange("p (j c) -> p j c", c=ROW)[:, 4 * g : 4 * g + 4, 0:P]

        def kwin(u, s):
            fb, g = units[u]
            return kv_of[fb][:, (4 * g + s) * P : (4 * g + s + 4) * P].rearrange("p (j c) -> p j c", c=P)

        def pe_project(u):
            fb, g = units[u]
            vps = psum.tile([P, 512], F32, name="vps", tag="vps", bufs=1)
            kps = psum.tile([P, 512], F32, name="kps", tag="kps", bufs=1)
            qps = psum.tile([P, 512], F32, name="qps", tag="qps", bufs=1)
            tiles[("v", u)] = vps
            tiles[("k", u)] = kps
            tiles[("q", u)] = qps
            project(vps[:], 3 * fb + 2, g)
            project(kps[:], 3 * fb + 1, g)
            project(qps[:], 3 * fb, g)

        def act_v_q(u):
            fb, g = units[u]
            vt = work.tile([P, 512], F32, name="vt", tag="vt", bufs=2)
            qs = work.tile([P, 512], F32, name="qs", tag="qs", bufs=2)
            tiles[("vt", u)] = vt
            tiles[("qs", u)] = qs
            nc.scalar.activation(
                out=vt[:], in_=tiles[("v", u)][:], func=IDENTITY, bias=consts[:, 8 + fb : 9 + fb], scale=1.0
            )
            nc.scalar.activation(
                out=qs[:], in_=tiles[("q", u)][:], func=IDENTITY, bias=consts[:, fb : fb + 1], scale=1.0
            )

        def dve_kv(u):
            fb, g = units[u]
            nc.vector.scalar_tensor_tensor(
                out=kv_of[fb][:, (1 + 4 * g) * P : (5 + 4 * g) * P],
                in0=tiles[("k", u)][:],
                scalar=consts[:, 4 + fb : 5 + fb],
                in1=tiles[("vt", u)][:],
                op0=ADD,
                op1=MULT,
            )

        def pe_q_transpose(u):
            qtp = psum.tile([P, 512], F32, name="qtp", tag="qtp", bufs=1)
            tiles[("qtp", u)] = qtp
            qs = tiles[("qs", u)]
            for jj in range(4):
                nc.tensor.transpose(qtp[:, jj * P : (jj + 1) * P], qs[:, jj * P : (jj + 1) * P], ident[:])

        def act_q_copy(u):
            qts = work.tile([P, 512], F32, name="qts", tag="qts", bufs=6)
            tiles[("qts", u)] = qts
            nc.scalar.copy(
                out=qts[:].rearrange("p (q jj s) -> p q jj s", q=16, jj=4, s=8),
                in_=tiles[("qtp", u)][:].rearrange("p (jj q s) -> p q jj s", jj=4, q=16, s=8),
            )

        def dve_columns(u):
            nc.vector.scalar_tensor_tensor(
                out=hwin(u, 4), in0=kwin(u, 0), scalar=a0s, in1=kwin(u, 1), op0=MULT, op1=ADD
            )
            nc.vector.scalar_tensor_tensor(
                out=hwin(u, 4), in0=kwin(u, 2), scalar=a2s, in1=hwin(u, 4), op0=MULT, op1=ADD
            )

        def act_scale_up(u):
            t0 = work.tile([P, 512], F32, name="t0", tag="t0", bufs=3)
            tiles[("t0", u)] = t0
            nc.scalar.activation(out=t0[:].rearrange("p (j c) -> p j c", c=P), in_=hwin(u, 0), func=COPY, scale=a0r)

        def dve_scale_down(u):
            t2 = work.tile([P, 512], F32, name="t2", tag="t2", bufs=3)
            tiles[("t2", u)] = t2
            nc.vector.tensor_scalar_mul(out=t2[:].rearrange("p (j c) -> p j c", c=P), in0=hwin(u, 8), scalar1=a2r)

        def pe_rows(u):
            fb, g = units[u]
            stp = psum.tile([P, 512], F32, name="stp", tag="stp", bufs=2)
            tiles[("stp", u)] = stp
            t0 = tiles[("t0", u)]
            t2 = tiles[("t2", u)]
            for jj in range(4):
                dst = stp[:, jj * P : (jj + 1) * P]
                c0 = (4 * g + jj) * ROW + 4
                nc.tensor.matmul(
                    out=dst, lhsT=hj_of[fb][:, c0 : c0 + P], rhs=ident[:], is_transpose=True, start=True, stop=False
                )
                nc.tensor.matmul(
                    out=dst, lhsT=t0[:, jj * P : (jj + 1) * P], rhs=ident[:], is_transpose=True, start=False, stop=False
                )
                nc.tensor.matmul(
                    out=dst, lhsT=t2[:, jj * P : (jj + 1) * P], rhs=ident[:], is_transpose=True, start=False, stop=True
                )

        def store(fb, ja, jb):
            if ja == 0 and jb == NJ:
                for b in range(NB):
                    nc.sync.dma_start(
                        out=out[b, 2 * fb : 2 * fb + 2].rearrange("c (i r) w -> i c (r w)", r=8),
                        in_=os_of[fb][b:P:4, :].rearrange("p (c f) -> p c f", c=2),
                    )
            else:
                for b in range(NB):
                    for c in range(2):
                        nc.sync.dma_start(
                            out=out[b, 2 * fb + c].rearrange("(i r) w -> i r w", r=8)[:, :, 8 * ja : 8 * jb],
                            in_=os_of[fb][b:P:4, c * 2048 : (c + 1) * 2048].rearrange("p (r w) -> p r w", r=8)[
                                :, :, 8 * ja : 8 * jb
                            ],
                        )

        def dve_final(u):
            fb, g = units[u]
            j0 = 4 * g
            nc.vector.tensor_tensor(
                out=os_of[fb][:].rearrange("p (q j s) -> p q j s", q=16, j=NJ, s=8)[:, :, j0 : j0 + 4, :],
                in0=tiles[("stp", u)][:].rearrange("p (jj q s) -> p q jj s", jj=4, q=16, s=8),
                in1=tiles[("qts", u)][:].rearrange("p (q jj s) -> p q jj s", q=16, jj=4, s=8),
                op=MULT,
            )
            if fb < NF - 1:
                if g == NG - 1:
                    store(fb, 0, NJ)
            elif g in LAST_STORES:
                store(fb, LAST_STORES[g], j0 + 4)

        def live(u):
            return 0 <= u < n_units

        for g in range(3):
            x_transpose(g)
            x_copy(g)
            if g >= 1:
                x_quantise(g - 1)
        for s in range(-1, n_units + 3):
            if live(s - 1):
                dve_scale_down(s - 1)
            if live(s + 1):
                if units[s + 1][1] == 0:
                    begin_block(units[s + 1][0])
                pe_project(s + 1)
            if live(s - 3):
                dve_final(s - 3)
            if live(s + 1):
                act_v_q(s + 1)
            if live(s - 2):
                pe_rows(s - 2)
            if live(s + 1):
                dve_kv(s + 1)
            if live(s - 1):
                act_scale_up(s - 1)
            if live(s + 1):
                pe_q_transpose(s + 1)
            if 0 <= s + 3 < NG and s + 3 >= 3:
                x_transpose(s + 3)
            if live(s):
                dve_columns(s)
            if 0 <= s + 2 < NG and s + 2 >= 2:
                x_quantise(s + 2)
            if live(s) and units[s][1] == 5 and units[s][0] + 1 < NF:
                w_quantise(units[s][0] + 1)
            if live(s + 1):
                act_q_copy(s + 1)
            if 0 <= s + 3 < NG and s + 3 >= 3:
                x_copy(s + 3)
            if live(s) and units[s][1] == 3 and units[s][0] + 1 < NF:
                w_transpose(units[s][0] + 1, nc.scalar.copy)
